import numpy as np
import ml_dtypes

BF16 = ml_dtypes.bfloat16


def bf(x):
    return np.asarray(x, np.float32).astype(BF16)


def f32(x):
    return np.asarray(x, np.float32)


def f64(x):
    return np.asarray(x).astype(np.float64)


def striped(idx):
    return np.tile(idx.reshape(-1, 16).T, (8, 1))


P, S, T, L, N = 128, 4096, 128, 16, 2048
ENL = 10.0


def sigmoid(v):
    return 1.0 / (1.0 + np.exp(-v))


def setup_inputs():
    z = np.random.standard_normal((P, S))
    sim = f32(ENL * z / np.sqrt((z * z).sum(axis=0, keepdims=True)))
    scores = f32(np.random.random((1, N)) < 0.6)
    slide = f32(-2.0 + 0.5 * np.random.standard_normal((1, S)))
    guess = f32(-2.0 + 0.5 * np.random.standard_normal((1, S)))
    return {"sim": sim, "scores": scores, "slide": slide, "guess": guess, "offs": striped(np.random.permutation(S)[:N])}


def reference(sim, scores, slide, guess, offs):
    idx = offs[:16].T.reshape(-1)
    a = f64(sim)
    w = np.exp(a[:, idx]).reshape(P, T, L)
    sc = f64(scores).reshape(1, T, L)
    prof = (w * sc).sum(axis=2) / w.sum(axis=2)
    v = np.exp(a)
    y = prof.T @ (v / v.sum(axis=0, keepdims=True))
    sl = sigmoid(f64(slide))
    gu = sigmoid(f64(guess))
    return (1.0 - sl) * y + gu * (1.0 - y)

@@ -1,0 +1,122 @@
+import concourse.mybir as mybir
+
+F32 = mybir.dt.float32
+BF16 = mybir.dt.bfloat16
+U16 = mybir.dt.uint16
+FN = mybir.ActivationFunctionType
+ALU = mybir.AluOpType
+AXIS_X = mybir.AxisListType.X
+
+P = 128
+S = 4096
+T = 128
+L = 16
+N = T * L
+SQ = 32
+QUADS = P // SQ
+BLOCKS = S // P
+SPAN = S // QUADS
+LOAD = 512
+PIECE = 512
+GROUPS = 4
+IN_GROUP = BLOCKS // GROUPS
+IN_BANK = 4
+
+FLOPS = 2 * P * T * S + 2 * P * S
+
+
+def tile_cicdm_net_kernel(tc, sim, scores, slide, guess, offs, out):
+    nc = tc.nc
+    with (
+        tc.tile_pool(name="held", bufs=1) as held,
+        tc.psum_pool(name="sums", bufs=1) as sums,
+        tc.psum_pool(name="banks", bufs=4) as banks,
+    ):
+        offsets = held.tile([P, N // 16], U16, name="offsets")
+        nc.sync.dma_start(offsets[:], offs)
+
+        logits = held.tile([P, 2 * SQ], F32, name="logits")
+        nc.sync.dma_start(logits[:, 0:SQ], slide.rearrange("o (q c) -> (o q) c", c=SQ))
+        nc.sync.dma_start(logits[:, SQ : 2 * SQ], guess.rearrange("o (q c) -> (o q) c", c=SQ))
+
+        table = held.tile([P, S], F32, name="table")
+        starts = [a * SPAN + half * LOAD for half in range(SPAN // LOAD) for a in range(QUADS)]
+        for j, lo in enumerate(starts):
+            queue = nc.sync if j % 2 == 0 else nc.scalar
+            queue.dma_start(table[:, lo : lo + LOAD], sim[:, lo : lo + LOAD])
+
+        score_rows = held.tile([P, N], F32, name="score_rows")
+        nc.sync.dma_start(score_rows[:], scores.rearrange("o n -> (o n)").partition_broadcast(P))
+
+        chance = held.tile([P, 2 * SQ], F32, name="chance", align_bytes=64)
+        nc.scalar.activation(chance[:], logits[:], FN.Exp, scale=-1.0)
+        nc.vector.tensor_scalar_add(chance[:], chance[:], 1.0)
+        nc.vector.reciprocal(chance[:], chance[:])
+        slope_rows = held.tile([P, SQ], F32, name="slope_rows", align_bytes=64)
+        nc.vector.tensor_tensor(slope_rows[:], chance[:, 0:SQ], chance[:, SQ : 2 * SQ], ALU.add)
+        nc.vector.tensor_scalar(slope_rows[:], slope_rows[:], -1.0, 1.0, ALU.mult, ALU.add)
+        slope = held.tile([P, BLOCKS], F32, name="slope", align_bytes=64)
+        floor = held.tile([P, BLOCKS], F32, name="floor", align_bytes=64)
+        nc.vector.transpose(slope[:], slope_rows[:])
+        nc.vector.transpose(floor[:], chance[:, SQ : 2 * SQ])
+
+        grown = held.tile([P, BLOCKS, P], BF16, name="grown")
+        for lo in starts:
+            a, k0 = lo // SPAN, (lo % SPAN) // SQ
+            nc.scalar.activation(
+                grown[:, k0 : k0 + LOAD // SQ, a * SQ : (a + 1) * SQ],
+                table[:, lo : lo + LOAD].rearrange("p (k c) -> p k c", c=SQ),
+                FN.Exp,
+            )
+
+        ones = held.tile([P, 1], BF16, name="ones")
+        nc.vector.memset(ones[:], 1.0)
+        total = sums.tile([P, BLOCKS], F32, name="total")
+        for k in range(BLOCKS):
+            nc.tensor.matmul(total[:, k : k + 1], grown[:, k, :], ones[:], start=True, stop=True)
+
+        picked = held.tile([P, N], F32, name="picked")
+        weight = held.tile([P, N], F32, name="weight")
+        scored = held.tile([P, N], F32, name="scored")
+        below = held.tile([P, T], F32, name="below")
+        above = held.tile([P, T], F32, name="above")
+        prof = held.tile([P, T], BF16, name="prof")
+        for piece in range(N // PIECE):
+            cols = slice(piece * PIECE, (piece + 1) * PIECE)
+            who = slice(piece * PIECE // L, (piece + 1) * PIECE // L)
+            listed = offsets[:, piece * PIECE // 16 : (piece + 1) * PIECE // 16]
+            nc.scalar.activation(picked[:, cols], table[:].indirect(listed), FN.Copy)
+            nc.scalar.activation(weight[:, cols], picked[:, cols], FN.Exp)
+            nc.vector.reduce_sum(below[:, who], weight[:, cols].rearrange("p (t l) -> p t l", l=L), axis=AXIS_X)
+            nc.vector.reciprocal(below[:, who], below[:, who])
+            nc.vector.tensor_mul(scored[:, cols], weight[:, cols], score_rows[:, cols])
+            nc.vector.reduce_sum(above[:, who], scored[:, cols].rearrange("p (t l) -> p t l", l=L), axis=AXIS_X)
+            nc.vector.tensor_mul(prof[:, who], above[:, who], below[:, who])
+
+        scale = held.tile([P, BLOCKS], F32, name="scale")
+        nc.vector.reciprocal(scale[:], total[:])
+        nc.vector.tensor_mul(scale[:], scale[:], slope[:])
+
+        lying = held.tile([P, GROUPS, QUADS, IN_GROUP, SQ], F32, name="lying", align_bytes=64)
+        upright = held.tile([P, GROUPS, QUADS, IN_GROUP * SQ], F32, name="upright", align_bytes=64)
+        out_view = out.rearrange("(b i) (a g m) -> a g i b m", i=SQ, a=QUADS, g=GROUPS)
+        for g in range(GROUPS):
+            for first in range(0, IN_GROUP, IN_BANK):
+                bank = banks.tile([P, IN_BANK, T], F32, name="bank")
+                for r in range(IN_BANK):
+                    h = first + r
+                    k = g * IN_GROUP + h
+                    nc.tensor.matmul(bank[:, r, :], grown[:, k, :], prof[:], start=True, stop=True)
+                    nc.scalar.activation(
+                        lying[:, g, :, h, :],
+                        bank[:, r, :].rearrange("p (b i) -> p b i", i=SQ),
+                        FN.Identity,
+                        bias=floor[:, k : k + 1],
+                        scale=scale[:, k : k + 1],
+                    )
+            nc.vector.transpose(
+                upright[:, g].rearrange("p b m -> p (b m)"),
+                lying[:, g].rearrange("p b h i -> p (b h i)"),
+            )
+            for a in range(QUADS):
+                nc.sync.dma_start(out_view[a, g], upright[a * SQ : (a + 1) * SQ, g])

@@ -17,10 +17,10 @@ QUADS = P // SQ
 BLOCKS = S // P
 SPAN = S // QUADS
 LOAD = 512
+EARLY = 6
 PIECE = 512
 GROUPS = 4
 IN_GROUP = BLOCKS // GROUPS
-IN_BANK = 4
 
 FLOPS = 2 * P * T * S + 2 * P * S
 
@@ -29,8 +29,9 @@ def tile_cicdm_net_kernel(tc, sim, scores, slide, guess, offs, out):
     nc = tc.nc
     with (
         tc.tile_pool(name="held", bufs=1) as held,
+        tc.tile_pool(name="turn", bufs=GROUPS) as turn,
         tc.psum_pool(name="sums", bufs=1) as sums,
-        tc.psum_pool(name="banks", bufs=4) as banks,
+        tc.psum_pool(name="banks", bufs=7) as banks,
     ):
         offsets = held.tile([P, N // 16], U16, name="offsets")
         nc.sync.dma_start(offsets[:], offs)
@@ -61,19 +62,30 @@ def tile_cicdm_net_kernel(tc, sim, scores, slide, guess, offs, out):
         nc.vector.transpose(floor[:], chance[:, SQ : 2 * SQ])
 
         grown = held.tile([P, BLOCKS, P], BF16, name="grown")
-        for lo in starts:
-            a, k0 = lo // SPAN, (lo % SPAN) // SQ
-            nc.scalar.activation(
-                grown[:, k0 : k0 + LOAD // SQ, a * SQ : (a + 1) * SQ],
-                table[:, lo : lo + LOAD].rearrange("p (k c) -> p k c", c=SQ),
-                FN.Exp,
-            )
+
+        def grow(loads):
+            for lo in loads:
+                a, k0 = lo // SPAN, (lo % SPAN) // SQ
+                nc.scalar.activation(
+                    grown[:, k0 : k0 + LOAD // SQ, a * SQ : (a + 1) * SQ],
+                    table[:, lo : lo + LOAD].rearrange("p (k c) -> p k c", c=SQ),
+                    FN.Exp,
+                )
 
         ones = held.tile([P, 1], BF16, name="ones")
         nc.vector.memset(ones[:], 1.0)
         total = sums.tile([P, BLOCKS], F32, name="total")
-        for k in range(BLOCKS):
-            nc.tensor.matmul(total[:, k : k + 1], grown[:, k, :], ones[:], start=True, stop=True)
+        scale = held.tile([P, BLOCKS], F32, name="scale")
+
+        def scales(blocks):
+            for k in blocks:
+                nc.tensor.matmul(total[:, k : k + 1], grown[:, k, :], ones[:], start=True, stop=True)
+            span = slice(blocks[0], blocks[-1] + 1)
+            nc.vector.reciprocal(scale[:, span], total[:, span])
+            nc.vector.tensor_mul(scale[:, span], scale[:, span], slope[:, span])
+
+        grow(starts[:EARLY])
+        scales(range(0, BLOCKS // 2))
 
         picked = held.tile([P, N], F32, name="picked")
         weight = held.tile([P, N], F32, name="weight")
@@ -89,34 +101,31 @@ def tile_cicdm_net_kernel(tc, sim, scores, slide, guess, offs, out):
             nc.scalar.activation(weight[:, cols], picked[:, cols], FN.Exp)
             nc.vector.reduce_sum(below[:, who], weight[:, cols].rearrange("p (t l) -> p t l", l=L), axis=AXIS_X)
             nc.vector.reciprocal(below[:, who], below[:, who])
-            nc.vector.tensor_mul(scored[:, cols], weight[:, cols], score_rows[:, cols])
+            nc.gpsimd.tensor_mul(scored[:, cols], weight[:, cols], score_rows[:, cols])
             nc.vector.reduce_sum(above[:, who], scored[:, cols].rearrange("p (t l) -> p t l", l=L), axis=AXIS_X)
             nc.vector.tensor_mul(prof[:, who], above[:, who], below[:, who])
 
-        scale = held.tile([P, BLOCKS], F32, name="scale")
-        nc.vector.reciprocal(scale[:], total[:])
-        nc.vector.tensor_mul(scale[:], scale[:], slope[:])
+        grow(starts[EARLY:])
+        scales(range(BLOCKS // 2, BLOCKS))
 
-        lying = held.tile([P, GROUPS, QUADS, IN_GROUP, SQ], F32, name="lying", align_bytes=64)
-        upright = held.tile([P, GROUPS, QUADS, IN_GROUP * SQ], F32, name="upright", align_bytes=64)
         out_view = out.rearrange("(b i) (a g m) -> a g i b m", i=SQ, a=QUADS, g=GROUPS)
         for g in range(GROUPS):
-            for first in range(0, IN_GROUP, IN_BANK):
-                bank = banks.tile([P, IN_BANK, T], F32, name="bank")
-                for r in range(IN_BANK):
-                    h = first + r
-                    k = g * IN_GROUP + h
-                    nc.tensor.matmul(bank[:, r, :], grown[:, k, :], prof[:], start=True, stop=True)
-                    nc.scalar.activation(
-                        lying[:, g, :, h, :],
-                        bank[:, r, :].rearrange("p (b i) -> p b i", i=SQ),
-                        FN.Identity,
-                        bias=floor[:, k : k + 1],
-                        scale=scale[:, k : k + 1],
-                    )
+            lying = turn.tile([P, QUADS, IN_GROUP, SQ], F32, name="lying", align_bytes=64)
+            for h in range(IN_GROUP):
+                k = g * IN_GROUP + h
+                product = banks.tile([P, T], F32, name="product")
+                nc.tensor.matmul(product[:], grown[:, k, :], prof[:], start=True, stop=True)
+                nc.scalar.activation(
+                    lying[:, :, h, :],
+                    product[:].rearrange("p (b i) -> p b i", i=SQ),
+                    FN.Identity,
+                    bias=floor[:, k : k + 1],
+                    scale=scale[:, k : k + 1],
+                )
+            upright = turn.tile([P, QUADS, IN_GROUP * SQ], F32, name="upright", align_bytes=64)
             nc.vector.transpose(
-                upright[:, g].rearrange("p b m -> p (b m)"),
-                lying[:, g].rearrange("p b h i -> p (b h i)"),
+                upright[:].rearrange("p b m -> p (b m)"),
+                lying[:].rearrange("p b h i -> p (b h i)"),
             )
             for a in range(QUADS):
-                nc.sync.dma_start(out_view[a, g], upright[a * SQ : (a + 1) * SQ, g])
+                nc.sync.dma_start(out_view[a, g], upright[a * SQ : (a + 1) * SQ])

@@ -19,6 +19,7 @@ SPAN = S // QUADS
 LOAD = 512
 EARLY = 6
 PIECE = 512
+PART = 256
 GROUPS = 4
 IN_GROUP = BLOCKS // GROUPS
 
@@ -94,16 +95,17 @@ def tile_cicdm_net_kernel(tc, sim, scores, slide, guess, offs, out):
         above = held.tile([P, T], F32, name="above")
         prof = held.tile([P, T], BF16, name="prof")
         for piece in range(N // PIECE):
-            cols = slice(piece * PIECE, (piece + 1) * PIECE)
-            who = slice(piece * PIECE // L, (piece + 1) * PIECE // L)
             listed = offsets[:, piece * PIECE // 16 : (piece + 1) * PIECE // 16]
-            nc.scalar.activation(picked[:, cols], table[:].indirect(listed), FN.Copy)
-            nc.scalar.activation(weight[:, cols], picked[:, cols], FN.Exp)
-            nc.vector.reduce_sum(below[:, who], weight[:, cols].rearrange("p (t l) -> p t l", l=L), axis=AXIS_X)
-            nc.vector.reciprocal(below[:, who], below[:, who])
-            nc.gpsimd.tensor_mul(scored[:, cols], weight[:, cols], score_rows[:, cols])
-            nc.vector.reduce_sum(above[:, who], scored[:, cols].rearrange("p (t l) -> p t l", l=L), axis=AXIS_X)
-            nc.vector.tensor_mul(prof[:, who], above[:, who], below[:, who])
+            nc.scalar.activation(picked[:, piece * PIECE : (piece + 1) * PIECE], table[:].indirect(listed), FN.Copy)
+            for lo in range(piece * PIECE, (piece + 1) * PIECE, PART):
+                cols = slice(lo, lo + PART)
+                who = slice(lo // L, (lo + PART) // L)
+                nc.scalar.activation(weight[:, cols], picked[:, cols], FN.Exp)
+                nc.gpsimd.tensor_mul(scored[:, cols], weight[:, cols], score_rows[:, cols])
+                nc.vector.reduce_sum(below[:, who], weight[:, cols].rearrange("p (t l) -> p t l", l=L), axis=AXIS_X)
+                nc.vector.reciprocal(below[:, who], below[:, who])
+                nc.vector.reduce_sum(above[:, who], scored[:, cols].rearrange("p (t l) -> p t l", l=L), axis=AXIS_X)
+                nc.vector.tensor_mul(prof[:, who], above[:, who], below[:, who])
 
         grow(starts[EARLY:])
         scales(range(BLOCKS // 2, BLOCKS))

@@ -1,4 +1,5 @@
 import concourse.mybir as mybir
+from concourse.masks import make_identity
 
 F32 = mybir.dt.float32
 BF16 = mybir.dt.bfloat16
@@ -12,16 +13,12 @@ S = 4096
 T = 128
 L = 16
 N = T * L
-SQ = 32
-QUADS = P // SQ
 BLOCKS = S // P
-SPAN = S // QUADS
-LOAD = 512
+WIDE = 512
+WIDES = S // WIDE
+IN_WIDE = WIDE // P
 EARLY = 6
 PIECE = 512
-PART = 256
-GROUPS = 4
-IN_GROUP = BLOCKS // GROUPS
 
 FLOPS = 2 * P * T * S + 2 * P * S
 
@@ -30,48 +27,48 @@ def tile_cicdm_net_kernel(tc, sim, scores, slide, guess, offs, out):
     nc = tc.nc
     with (
         tc.tile_pool(name="held", bufs=1) as held,
-        tc.tile_pool(name="turn", bufs=GROUPS) as turn,
+        tc.tile_pool(name="work", bufs=WIDES) as work,
         tc.psum_pool(name="sums", bufs=1) as sums,
-        tc.psum_pool(name="banks", bufs=7) as banks,
+        tc.psum_pool(name="products", bufs=4) as products,
+        tc.psum_pool(name="turns", bufs=2) as turns,
     ):
         offsets = held.tile([P, N // 16], U16, name="offsets")
         nc.sync.dma_start(offsets[:], offs)
 
-        logits = held.tile([P, 2 * SQ], F32, name="logits")
-        nc.sync.dma_start(logits[:, 0:SQ], slide.rearrange("o (q c) -> (o q) c", c=SQ))
-        nc.sync.dma_start(logits[:, SQ : 2 * SQ], guess.rearrange("o (q c) -> (o q) c", c=SQ))
+        logits = held.tile([2 * BLOCKS, P], F32, name="logits")
+        nc.sync.dma_start(logits[0:BLOCKS, :], slide.rearrange("o (k q) -> (o k) q", q=P))
+        nc.sync.dma_start(logits[BLOCKS : 2 * BLOCKS, :], guess.rearrange("o (k q) -> (o k) q", q=P))
 
         table = held.tile([P, S], F32, name="table")
-        starts = [a * SPAN + half * LOAD for half in range(SPAN // LOAD) for a in range(QUADS)]
-        for j, lo in enumerate(starts):
-            queue = nc.sync if j % 2 == 0 else nc.scalar
-            queue.dma_start(table[:, lo : lo + LOAD], sim[:, lo : lo + LOAD])
+        for w in range(WIDES):
+            queue = nc.sync if w % 2 == 0 else nc.scalar
+            queue.dma_start(table[:, w * WIDE : (w + 1) * WIDE], sim[:, w * WIDE : (w + 1) * WIDE])
 
         score_rows = held.tile([P, N], F32, name="score_rows")
         nc.sync.dma_start(score_rows[:], scores.rearrange("o n -> (o n)").partition_broadcast(P))
 
-        chance = held.tile([P, 2 * SQ], F32, name="chance", align_bytes=64)
-        nc.scalar.activation(chance[:], logits[:], FN.Exp, scale=-1.0)
-        nc.vector.tensor_scalar_add(chance[:], chance[:], 1.0)
-        nc.vector.reciprocal(chance[:], chance[:])
-        slope_rows = held.tile([P, SQ], F32, name="slope_rows", align_bytes=64)
-        nc.vector.tensor_tensor(slope_rows[:], chance[:, 0:SQ], chance[:, SQ : 2 * SQ], ALU.add)
-        nc.vector.tensor_scalar(slope_rows[:], slope_rows[:], -1.0, 1.0, ALU.mult, ALU.add)
-        slope = held.tile([P, BLOCKS], F32, name="slope", align_bytes=64)
-        floor = held.tile([P, BLOCKS], F32, name="floor", align_bytes=64)
-        nc.vector.transpose(slope[:], slope_rows[:])
-        nc.vector.transpose(floor[:], chance[:, SQ : 2 * SQ])
+        identity = held.tile([P, P], F32, name="identity")
+        make_identity(nc, identity[:])
 
-        grown = held.tile([P, BLOCKS, P], BF16, name="grown")
+        chance_rows = held.tile([2 * BLOCKS, P], F32, name="chance_rows")
+        nc.scalar.activation(chance_rows[:], logits[:], FN.Exp, scale=-1.0)
+        nc.vector.tensor_scalar_add(chance_rows[:], chance_rows[:], 1.0)
+        nc.vector.reciprocal(chance_rows[:], chance_rows[:])
+        chance_turned = sums.tile([P, 2 * BLOCKS], F32, name="chance_turned")
+        nc.tensor.transpose(chance_turned[:], chance_rows[:], identity[0 : 2 * BLOCKS, 0 : 2 * BLOCKS])
+        chance = held.tile([P, 2 * BLOCKS], F32, name="chance")
+        nc.vector.tensor_copy(chance[:], chance_turned[:])
+        floor = chance[:, BLOCKS : 2 * BLOCKS]
+        slope = held.tile([P, BLOCKS], F32, name="slope")
+        nc.vector.tensor_tensor(slope[:], chance[:, 0:BLOCKS], floor, ALU.add)
+        nc.vector.tensor_scalar(slope[:], slope[:], -1.0, 1.0, ALU.mult, ALU.add)
 
-        def grow(loads):
-            for lo in loads:
-                a, k0 = lo // SPAN, (lo % SPAN) // SQ
-                nc.scalar.activation(
-                    grown[:, k0 : k0 + LOAD // SQ, a * SQ : (a + 1) * SQ],
-                    table[:, lo : lo + LOAD].rearrange("p (k c) -> p k c", c=SQ),
-                    FN.Exp,
-                )
+        grown = held.tile([P, S], BF16, name="grown")
+
+        def grow(wides):
+            for w in wides:
+                cols = slice(w * WIDE, (w + 1) * WIDE)
+                nc.scalar.activation(grown[:, cols], table[:, cols], FN.Exp)
 
         ones = held.tile([P, 1], BF16, name="ones")
         nc.vector.memset(ones[:], 1.0)
@@ -80,13 +77,13 @@ def tile_cicdm_net_kernel(tc, sim, scores, slide, guess, offs, out):
 
         def scales(blocks):
             for k in blocks:
-                nc.tensor.matmul(total[:, k : k + 1], grown[:, k, :], ones[:], start=True, stop=True)
+                nc.tensor.matmul(total[:, k : k + 1], grown[:, k * P : (k + 1) * P], ones[:], start=True, stop=True)
             span = slice(blocks[0], blocks[-1] + 1)
             nc.vector.reciprocal(scale[:, span], total[:, span])
             nc.vector.tensor_mul(scale[:, span], scale[:, span], slope[:, span])
 
-        grow(starts[:EARLY])
-        scales(range(0, BLOCKS // 2))
+        grow(range(EARLY))
+        scales(range(EARLY * IN_WIDE))
 
         picked = held.tile([P, N], F32, name="picked")
         weight = held.tile([P, N], F32, name="weight")
@@ -95,39 +92,41 @@ def tile_cicdm_net_kernel(tc, sim, scores, slide, guess, offs, out):
         above = held.tile([P, T], F32, name="above")
         prof = held.tile([P, T], BF16, name="prof")
         for piece in range(N // PIECE):
+            cols = slice(piece * PIECE, (piece + 1) * PIECE)
+            who = slice(piece * PIECE // L, (piece + 1) * PIECE // L)
             listed = offsets[:, piece * PIECE // 16 : (piece + 1) * PIECE // 16]
-            nc.scalar.activation(picked[:, piece * PIECE : (piece + 1) * PIECE], table[:].indirect(listed), FN.Copy)
-            for lo in range(piece * PIECE, (piece + 1) * PIECE, PART):
-                cols = slice(lo, lo + PART)
-                who = slice(lo // L, (lo + PART) // L)
-                nc.scalar.activation(weight[:, cols], picked[:, cols], FN.Exp)
-                nc.gpsimd.tensor_mul(scored[:, cols], weight[:, cols], score_rows[:, cols])
-                nc.vector.reduce_sum(below[:, who], weight[:, cols].rearrange("p (t l) -> p t l", l=L), axis=AXIS_X)
-                nc.vector.reciprocal(below[:, who], below[:, who])
-                nc.vector.reduce_sum(above[:, who], scored[:, cols].rearrange("p (t l) -> p t l", l=L), axis=AXIS_X)
-                nc.vector.tensor_mul(prof[:, who], above[:, who], below[:, who])
+            nc.scalar.activation(picked[:, cols], table[:].indirect(listed), FN.Copy)
+            nc.scalar.activation(weight[:, cols], picked[:, cols], FN.Exp)
+            nc.vector.reduce_sum(below[:, who], weight[:, cols].rearrange("p (t l) -> p t l", l=L), axis=AXIS_X)
+            nc.vector.reciprocal(below[:, who], below[:, who])
+            nc.gpsimd.tensor_mul(scored[:, cols], weight[:, cols], score_rows[:, cols])
+            nc.vector.reduce_sum(above[:, who], scored[:, cols].rearrange("p (t l) -> p t l", l=L), axis=AXIS_X)
+            nc.vector.tensor_mul(prof[:, who], above[:, who], below[:, who])
 
-        grow(starts[EARLY:])
-        scales(range(BLOCKS // 2, BLOCKS))
+        grow(range(EARLY, WIDES))
+        scales(range(EARLY * IN_WIDE, BLOCKS))
 
-        out_view = out.rearrange("(b i) (a g m) -> a g i b m", i=SQ, a=QUADS, g=GROUPS)
-        for g in range(GROUPS):
-            lying = turn.tile([P, QUADS, IN_GROUP, SQ], F32, name="lying", align_bytes=64)
-            for h in range(IN_GROUP):
-                k = g * IN_GROUP + h
-                product = banks.tile([P, T], F32, name="product")
-                nc.tensor.matmul(product[:], grown[:, k, :], prof[:], start=True, stop=True)
+        def multiply(w):
+            lying = work.tile([P, IN_WIDE, T], F32, name="lying")
+            for r in range(IN_WIDE):
+                k = w * IN_WIDE + r
+                product = products.tile([P, T], F32, name="product")
+                nc.tensor.matmul(product[:], grown[:, k * P : (k + 1) * P], prof[:], start=True, stop=True)
                 nc.scalar.activation(
-                    lying[:, :, h, :],
-                    product[:].rearrange("p (b i) -> p b i", i=SQ),
-                    FN.Identity,
-                    bias=floor[:, k : k + 1],
-                    scale=scale[:, k : k + 1],
+                    lying[:, r, :], product[:], FN.Identity, bias=floor[:, k : k + 1], scale=scale[:, k : k + 1]
                 )
-            upright = turn.tile([P, QUADS, IN_GROUP * SQ], F32, name="upright", align_bytes=64)
-            nc.vector.transpose(
-                upright[:].rearrange("p b m -> p (b m)"),
-                lying[:].rearrange("p b h i -> p (b h i)"),
-            )
-            for a in range(QUADS):
-                nc.sync.dma_start(out_view[a, g], upright[a * SQ : (a + 1) * SQ])
+            return lying
+
+        def turn(w, lying):
+            turned = turns.tile([P, IN_WIDE, P], F32, name="turned")
+            for r in range(IN_WIDE):
+                nc.tensor.transpose(turned[:, r, :], lying[:, r, :], identity[:])
+            upright = work.tile([P, WIDE], F32, name="upright")
+            nc.vector.tensor_copy(upright[:], turned[:].rearrange("p r q -> p (r q)"))
+            nc.sync.dma_start(out[:, w * WIDE : (w + 1) * WIDE], upright[:])
+
+        lying = multiply(0)
+        for w in range(WIDES):
+            ahead = multiply(w + 1) if w + 1 < WIDES else None
+            turn(w, lying)
+            lying = ahead

@@ -17,8 +17,9 @@ BLOCKS = S // P
 WIDE = 512
 WIDES = S // WIDE
 IN_WIDE = WIDE // P
-EARLY = 6
+EARLY = 3
 PIECE = 512
+AHEAD = 2
 
 FLOPS = 2 * P * T * S + 2 * P * S
 
@@ -29,8 +30,8 @@ def tile_cicdm_net_kernel(tc, sim, scores, slide, guess, offs, out):
         tc.tile_pool(name="held", bufs=1) as held,
         tc.tile_pool(name="work", bufs=WIDES) as work,
         tc.psum_pool(name="sums", bufs=1) as sums,
-        tc.psum_pool(name="products", bufs=4) as products,
-        tc.psum_pool(name="turns", bufs=2) as turns,
+        tc.psum_pool(name="products", bufs=3) as products,
+        tc.psum_pool(name="turns", bufs=3) as turns,
     ):
         offsets = held.tile([P, N // 16], U16, name="offsets")
         nc.sync.dma_start(offsets[:], offs)
@@ -45,7 +46,9 @@ def tile_cicdm_net_kernel(tc, sim, scores, slide, guess, offs, out):
             queue.dma_start(table[:, w * WIDE : (w + 1) * WIDE], sim[:, w * WIDE : (w + 1) * WIDE])
 
         score_rows = held.tile([P, N], F32, name="score_rows")
-        nc.sync.dma_start(score_rows[:], scores.rearrange("o n -> (o n)").partition_broadcast(P))
+        for piece in range(N // PIECE):
+            cols = slice(piece * PIECE, (piece + 1) * PIECE)
+            nc.sync.dma_start(score_rows[:, cols], scores[:, cols].rearrange("o n -> (o n)").partition_broadcast(P))
 
         identity = held.tile([P, P], F32, name="identity")
         make_identity(nc, identity[:])
@@ -108,12 +111,14 @@ def tile_cicdm_net_kernel(tc, sim, scores, slide, guess, offs, out):
 
         def multiply(w):
             lying = work.tile([P, IN_WIDE, T], F32, name="lying")
+            product = products.tile([P, IN_WIDE, T], F32, name="product")
             for r in range(IN_WIDE):
                 k = w * IN_WIDE + r
-                product = products.tile([P, T], F32, name="product")
-                nc.tensor.matmul(product[:], grown[:, k * P : (k + 1) * P], prof[:], start=True, stop=True)
+                nc.tensor.matmul(product[:, r, :], grown[:, k * P : (k + 1) * P], prof[:], start=True, stop=True)
+            for r in range(IN_WIDE):
+                k = w * IN_WIDE + r
                 nc.scalar.activation(
-                    lying[:, r, :], product[:], FN.Identity, bias=floor[:, k : k + 1], scale=scale[:, k : k + 1]
+                    lying[:, r, :], product[:, r, :], FN.Identity, bias=floor[:, k : k + 1], scale=scale[:, k : k + 1]
                 )
             return lying
 
@@ -125,8 +130,8 @@ def tile_cicdm_net_kernel(tc, sim, scores, slide, guess, offs, out):
             nc.vector.tensor_copy(upright[:], turned[:].rearrange("p r q -> p (r q)"))
             nc.sync.dma_start(out[:, w * WIDE : (w + 1) * WIDE], upright[:])
 
-        lying = multiply(0)
+        lyings = [multiply(w) for w in range(AHEAD)]
         for w in range(WIDES):
-            ahead = multiply(w + 1) if w + 1 < WIDES else None
-            turn(w, lying)
-            lying = ahead
+            if w + AHEAD < WIDES:
+                lyings.append(multiply(w + AHEAD))
+            turn(w, lyings[w])

@@ -18,7 +18,7 @@ WIDE = 512
 WIDES = S // WIDE
 IN_WIDE = WIDE // P
 EARLY = 3
-PIECE = 512
+PIECE = 256
 AHEAD = 2
 
 FLOPS = 2 * P * T * S + 2 * P * S
@@ -46,8 +46,8 @@ def tile_cicdm_net_kernel(tc, sim, scores, slide, guess, offs, out):
             queue.dma_start(table[:, w * WIDE : (w + 1) * WIDE], sim[:, w * WIDE : (w + 1) * WIDE])
 
         score_rows = held.tile([P, N], F32, name="score_rows")
-        for piece in range(N // PIECE):
-            cols = slice(piece * PIECE, (piece + 1) * PIECE)
+        for w in range(N // WIDE):
+            cols = slice(w * WIDE, (w + 1) * WIDE)
             nc.sync.dma_start(score_rows[:, cols], scores[:, cols].rearrange("o n -> (o n)").partition_broadcast(P))
 
         identity = held.tile([P, P], F32, name="identity")

@@ -17,6 +17,7 @@ BLOCKS = S // P
 WIDE = 512
 WIDES = S // WIDE
 IN_WIDE = WIDE // P
+LOAD = 1024
 EARLY = 3
 PIECE = 256
 AHEAD = 2
@@ -41,9 +42,9 @@ def tile_cicdm_net_kernel(tc, sim, scores, slide, guess, offs, out):
         nc.sync.dma_start(logits[BLOCKS : 2 * BLOCKS, :], guess.rearrange("o (k q) -> (o k) q", q=P))
 
         table = held.tile([P, S], F32, name="table")
-        for w in range(WIDES):
-            queue = nc.sync if w % 2 == 0 else nc.scalar
-            queue.dma_start(table[:, w * WIDE : (w + 1) * WIDE], sim[:, w * WIDE : (w + 1) * WIDE])
+        for piece in range(S // LOAD):
+            queue = nc.sync if piece % 2 == 0 else nc.scalar
+            queue.dma_start(table[:, piece * LOAD : (piece + 1) * LOAD], sim[:, piece * LOAD : (piece + 1) * LOAD])
 
         score_rows = held.tile([P, N], F32, name="score_rows")
         for w in range(N // WIDE):

@@ -47,8 +47,8 @@ def tile_cicdm_net_kernel(tc, sim, scores, slide, guess, offs, out):
             queue.dma_start(table[:, piece * LOAD : (piece + 1) * LOAD], sim[:, piece * LOAD : (piece + 1) * LOAD])
 
         score_rows = held.tile([P, N], F32, name="score_rows")
-        for w in range(N // WIDE):
-            cols = slice(w * WIDE, (w + 1) * WIDE)
+        for piece in range(N // LOAD):
+            cols = slice(piece * LOAD, (piece + 1) * LOAD)
             nc.sync.dma_start(score_rows[:, cols], scores[:, cols].rearrange("o n -> (o n)").partition_broadcast(P))
 
         identity = held.tile([P, P], F32, name="identity")

@@ -47,9 +47,7 @@ def tile_cicdm_net_kernel(tc, sim, scores, slide, guess, offs, out):
             queue.dma_start(table[:, piece * LOAD : (piece + 1) * LOAD], sim[:, piece * LOAD : (piece + 1) * LOAD])
 
         score_rows = held.tile([P, N], F32, name="score_rows")
-        for piece in range(N // LOAD):
-            cols = slice(piece * LOAD, (piece + 1) * LOAD)
-            nc.sync.dma_start(score_rows[:, cols], scores[:, cols].rearrange("o n -> (o n)").partition_broadcast(P))
+        nc.sync.dma_start(score_rows[:], scores.rearrange("o n -> (o n)").partition_broadcast(P))
 
         identity = held.tile([P, P], F32, name="identity")
         make_identity(nc, identity[:])

@@ -116,8 +116,8 @@ def tile_cicdm_net_kernel(tc, sim, scores, slide, guess, offs, out):
                 nc.tensor.matmul(product[:, r, :], grown[:, k * P : (k + 1) * P], prof[:], start=True, stop=True)
             for r in range(IN_WIDE):
                 k = w * IN_WIDE + r
-                nc.scalar.activation(
-                    lying[:, r, :], product[:, r, :], FN.Identity, bias=floor[:, k : k + 1], scale=scale[:, k : k + 1]
+                nc.vector.tensor_scalar(
+                    lying[:, r, :], product[:, r, :], scale[:, k : k + 1], floor[:, k : k + 1], ALU.mult, ALU.add
                 )
             return lying
 
@@ -126,7 +126,7 @@ def tile_cicdm_net_kernel(tc, sim, scores, slide, guess, offs, out):
             for r in range(IN_WIDE):
                 nc.tensor.transpose(turned[:, r, :], lying[:, r, :], identity[:])
             upright = work.tile([P, WIDE], F32, name="upright")
-            nc.vector.tensor_copy(upright[:], turned[:].rearrange("p r q -> p (r q)"))
+            nc.scalar.copy(upright[:], turned[:].rearrange("p r q -> p (r q)"))
             nc.sync.dma_start(out[:, w * WIDE : (w + 1) * WIDE], upright[:])
 
         lyings = [multiply(w) for w in range(AHEAD)]

@@ -18,9 +18,10 @@ WIDE = 512
 WIDES = S // WIDE
 IN_WIDE = WIDE // P
 LOAD = 1024
-EARLY = 3
+EARLY = 4
 PIECE = 256
-AHEAD = 2
+FIRST = 3 * T // 4
+HELD = 4
 
 FLOPS = 2 * P * T * S + 2 * P * S
 
@@ -31,7 +32,7 @@ def tile_cicdm_net_kernel(tc, sim, scores, slide, guess, offs, out):
         tc.tile_pool(name="held", bufs=1) as held,
         tc.tile_pool(name="work", bufs=WIDES) as work,
         tc.psum_pool(name="sums", bufs=1) as sums,
-        tc.psum_pool(name="products", bufs=3) as products,
+        tc.psum_pool(name="products", bufs=HELD) as products,
         tc.psum_pool(name="turns", bufs=3) as turns,
     ):
         offsets = held.tile([P, N // 16], U16, name="offsets")
@@ -56,7 +57,7 @@ def tile_cicdm_net_kernel(tc, sim, scores, slide, guess, offs, out):
         nc.scalar.activation(chance_rows[:], logits[:], FN.Exp, scale=-1.0)
         nc.vector.tensor_scalar_add(chance_rows[:], chance_rows[:], 1.0)
         nc.vector.reciprocal(chance_rows[:], chance_rows[:])
-        chance_turned = sums.tile([P, 2 * BLOCKS], F32, name="chance_turned")
+        chance_turned = turns.tile([P, 2 * BLOCKS], F32, name="chance_turned", tag="turned")
         nc.tensor.transpose(chance_turned[:], chance_rows[:], identity[0 : 2 * BLOCKS, 0 : 2 * BLOCKS])
         chance = held.tile([P, 2 * BLOCKS], F32, name="chance")
         nc.vector.tensor_copy(chance[:], chance_turned[:])
@@ -87,12 +88,20 @@ def tile_cicdm_net_kernel(tc, sim, scores, slide, guess, offs, out):
         grow(range(EARLY))
         scales(range(EARLY * IN_WIDE))
 
+        def multiply(w, product, students):
+            for r in range(IN_WIDE):
+                k = w * IN_WIDE + r
+                nc.tensor.matmul(
+                    product[:, r, students], grown[:, k * P : (k + 1) * P], prof[:, students], start=True, stop=True
+                )
+
         picked = held.tile([P, N], F32, name="picked")
         weight = held.tile([P, N], F32, name="weight")
         scored = held.tile([P, N], F32, name="scored")
         below = held.tile([P, T], F32, name="below")
         above = held.tile([P, T], F32, name="above")
         prof = held.tile([P, T], BF16, name="prof")
+        begun = []
         for piece in range(N // PIECE):
             cols = slice(piece * PIECE, (piece + 1) * PIECE)
             who = slice(piece * PIECE // L, (piece + 1) * PIECE // L)
@@ -104,16 +113,17 @@ def tile_cicdm_net_kernel(tc, sim, scores, slide, guess, offs, out):
             nc.gpsimd.tensor_mul(scored[:, cols], weight[:, cols], score_rows[:, cols])
             nc.vector.reduce_sum(above[:, who], scored[:, cols].rearrange("p (t l) -> p t l", l=L), axis=AXIS_X)
             nc.vector.tensor_mul(prof[:, who], above[:, who], below[:, who])
+            if who.stop == FIRST:
+                for w in range(HELD):
+                    product = products.tile([P, IN_WIDE, T], F32, name="product")
+                    multiply(w, product, slice(0, FIRST))
+                    begun.append(product)
 
         grow(range(EARLY, WIDES))
         scales(range(EARLY * IN_WIDE, BLOCKS))
 
-        def multiply(w):
+        def scale_out(w, product):
             lying = work.tile([P, IN_WIDE, T], F32, name="lying")
-            product = products.tile([P, IN_WIDE, T], F32, name="product")
-            for r in range(IN_WIDE):
-                k = w * IN_WIDE + r
-                nc.tensor.matmul(product[:, r, :], grown[:, k * P : (k + 1) * P], prof[:], start=True, stop=True)
             for r in range(IN_WIDE):
                 k = w * IN_WIDE + r
                 nc.vector.tensor_scalar(
@@ -129,8 +139,13 @@ def tile_cicdm_net_kernel(tc, sim, scores, slide, guess, offs, out):
             nc.scalar.copy(upright[:], turned[:].rearrange("p r q -> p (r q)"))
             nc.sync.dma_start(out[:, w * WIDE : (w + 1) * WIDE], upright[:])
 
-        lyings = [multiply(w) for w in range(AHEAD)]
+        lyings = []
+        for w in range(HELD):
+            multiply(w, begun[w], slice(FIRST, T))
+            lyings.append(scale_out(w, begun[w]))
         for w in range(WIDES):
-            if w + AHEAD < WIDES:
-                lyings.append(multiply(w + AHEAD))
             turn(w, lyings[w])
+            if w + HELD < WIDES:
+                product = products.tile([P, IN_WIDE, T], F32, name="product")
+                multiply(w + HELD, product, slice(0, T))
+                lyings.append(scale_out(w + HELD, product))

import concourse.mybir as mybir
from concourse.masks import make_identity

F32 = mybir.dt.float32
BF16 = mybir.dt.bfloat16
U16 = mybir.dt.uint16
FN = mybir.ActivationFunctionType
ALU = mybir.AluOpType
AXIS_X = mybir.AxisListType.X

P = 128
S = 4096
T = 128
L = 16
N = T * L
BLOCKS = S // P
WIDE = 512
WIDES = S // WIDE
IN_WIDE = WIDE // P
LOAD = 1024
EARLY = 4
PIECE = 256
FIRST = 3 * T // 4
HELD = 4

FLOPS = 2 * P * T * S + 2 * P * S


def tile_cicdm_net_kernel(tc, sim, scores, slide, guess, offs, out):
    nc = tc.nc
    with (
        tc.tile_pool(name="held", bufs=1) as held,
        tc.tile_pool(name="work", bufs=WIDES) as work,
        tc.psum_pool(name="sums", bufs=1) as sums,
        tc.psum_pool(name="products", bufs=HELD) as products,
        tc.psum_pool(name="turns", bufs=3) as turns,
    ):
        offsets = held.tile([P, N // 16], U16, name="offsets")
        nc.sync.dma_start(offsets[:], offs)

        logits = held.tile([2 * BLOCKS, P], F32, name="logits")
        nc.sync.dma_start(logits[0:BLOCKS, :], slide.rearrange("o (k q) -> (o k) q", q=P))
        nc.sync.dma_start(logits[BLOCKS : 2 * BLOCKS, :], guess.rearrange("o (k q) -> (o k) q", q=P))

        table = held.tile([P, S], F32, name="table")
        for piece in range(S // LOAD):
            queue = nc.sync if piece % 2 == 0 else nc.scalar
            queue.dma_start(table[:, piece * LOAD : (piece + 1) * LOAD], sim[:, piece * LOAD : (piece + 1) * LOAD])

        score_rows = held.tile([P, N], F32, name="score_rows")
        nc.sync.dma_start(score_rows[:], scores.rearrange("o n -> (o n)").partition_broadcast(P))

        identity = held.tile([P, P], F32, name="identity")
        make_identity(nc, identity[:])

        chance_rows = held.tile([2 * BLOCKS, P], F32, name="chance_rows")
        nc.scalar.activation(chance_rows[:], logits[:], FN.Exp, scale=-1.0)
        nc.vector.tensor_scalar_add(chance_rows[:], chance_rows[:], 1.0)
        nc.vector.reciprocal(chance_rows[:], chance_rows[:])
        chance_turned = turns.tile([P, 2 * BLOCKS], F32, name="chance_turned", tag="turned")
        nc.tensor.transpose(chance_turned[:], chance_rows[:], identity[0 : 2 * BLOCKS, 0 : 2 * BLOCKS])
        chance = held.tile([P, 2 * BLOCKS], F32, name="chance")
        nc.vector.tensor_copy(chance[:], chance_turned[:])
        floor = chance[:, BLOCKS : 2 * BLOCKS]
        slope = held.tile([P, BLOCKS], F32, name="slope")
        nc.vector.tensor_tensor(slope[:], chance[:, 0:BLOCKS], floor, ALU.add)
        nc.vector.tensor_scalar(slope[:], slope[:], -1.0, 1.0, ALU.mult, ALU.add)

        grown = held.tile([P, S], BF16, name="grown")

        def grow(wides):
            for w in wides:
                cols = slice(w * WIDE, (w + 1) * WIDE)
                nc.scalar.activation(grown[:, cols], table[:, cols], FN.Exp)

        ones = held.tile([P, 1], BF16, name="ones")
        nc.vector.memset(ones[:], 1.0)
        total = sums.tile([P, BLOCKS], F32, name="total")
        scale = held.tile([P, BLOCKS], F32, name="scale")

        def scales(blocks):
            for k in blocks:
                nc.tensor.matmul(total[:, k : k + 1], grown[:, k * P : (k + 1) * P], ones[:], start=True, stop=True)
            span = slice(blocks[0], blocks[-1] + 1)
            nc.vector.reciprocal(scale[:, span], total[:, span])
            nc.vector.tensor_mul(scale[:, span], scale[:, span], slope[:, span])

        grow(range(EARLY))
        scales(range(EARLY * IN_WIDE))

        def multiply(w, product, students):
            for r in range(IN_WIDE):
                k = w * IN_WIDE + r
                nc.tensor.matmul(
                    product[:, r, students], grown[:, k * P : (k + 1) * P], prof[:, students], start=True, stop=True
                )

        picked = held.tile([P, N], F32, name="picked")
        weight = held.tile([P, N], F32, name="weight")
        scored = held.tile([P, N], F32, name="scored")
        below = held.tile([P, T], F32, name="below")
        above = held.tile([P, T], F32, name="above")
        prof = held.tile([P, T], BF16, name="prof")
        begun = []
        for piece in range(N // PIECE):
            cols = slice(piece * PIECE, (piece + 1) * PIECE)
            who = slice(piece * PIECE // L, (piece + 1) * PIECE // L)
            listed = offsets[:, piece * PIECE // 16 : (piece + 1) * PIECE // 16]
            nc.scalar.activation(picked[:, cols], table[:].indirect(listed), FN.Copy)
            nc.scalar.activation(weight[:, cols], picked[:, cols], FN.Exp)
            nc.vector.reduce_sum(below[:, who], weight[:, cols].rearrange("p (t l) -> p t l", l=L), axis=AXIS_X)
            nc.vector.reciprocal(below[:, who], below[:, who])
            nc.gpsimd.tensor_mul(scored[:, cols], weight[:, cols], score_rows[:, cols])
            nc.vector.reduce_sum(above[:, who], scored[:, cols].rearrange("p (t l) -> p t l", l=L), axis=AXIS_X)
            nc.vector.tensor_mul(prof[:, who], above[:, who], below[:, who])
            if who.stop == FIRST:
                for w in range(HELD):
                    product = products.tile([P, IN_WIDE, T], F32, name="product")
                    multiply(w, product, slice(0, FIRST))
                    begun.append(product)

        grow(range(EARLY, WIDES))
        scales(range(EARLY * IN_WIDE, BLOCKS))

        def scale_out(w, product):
            lying = work.tile([P, IN_WIDE, T], F32, name="lying")
            for r in range(IN_WIDE):
                k = w * IN_WIDE + r
                nc.vector.tensor_scalar(
                    lying[:, r, :], product[:, r, :], scale[:, k : k + 1], floor[:, k : k + 1], ALU.mult, ALU.add
                )
            return lying

        def turn(w, lying):
            turned = turns.tile([P, IN_WIDE, P], F32, name="turned")
            for r in range(IN_WIDE):
                nc.tensor.transpose(turned[:, r, :], lying[:, r, :], identity[:])
            upright = work.tile([P, WIDE], F32, name="upright")
            nc.scalar.copy(upright[:], turned[:].rearrange("p r q -> p (r q)"))
            nc.sync.dma_start(out[:, w * WIDE : (w + 1) * WIDE], upright[:])

        lyings = []
        for w in range(HELD):
            multiply(w, begun[w], slice(FIRST, T))
            lyings.append(scale_out(w, begun[w]))
        for w in range(WIDES):
            turn(w, lyings[w])
            if w + HELD < WIDES:
                product = products.tile([P, IN_WIDE, T], F32, name="product")
                multiply(w + HELD, product, slice(0, T))
                lyings.append(scale_out(w + HELD, product))
